import numpy as np
import ml_dtypes


def mxq(x, axis, fmt="e4m3"):
    dtype, down = {"e4m3": (ml_dtypes.float8_e4m3fn, 7), "e5m2": (ml_dtypes.float8_e5m2, 14)}[fmt]
    v = np.moveaxis(np.asarray(x, np.float32).astype(ml_dtypes.bfloat16).astype(np.float64), axis, -1)
    blocks = v.reshape(v.shape[:-1] + (-1, 32))
    amax = np.abs(blocks).max(-1, keepdims=True)
    byte = np.maximum(np.where(amax > 0, np.frexp(amax)[1] - 1 + 127, 0) - down, 1)
    scale = np.exp2(byte - 127.0)
    codes = (blocks / scale).astype(np.float32).astype(dtype).astype(np.float64)
    return np.moveaxis((codes * scale).reshape(v.shape), -1, axis)


WIDE = False


def mx_kscale(k):
    if not WIDE:
        return np.ones(k)
    levels = np.array([10, -10, 5, -5, 0])
    a = np.random.permutation(np.resize(levels, k // 512 * 4)).reshape(k // 512, 4)
    idx = np.arange(k)
    return np.exp2(a[idx // 512, idx % 128 // 32])


BF16 = ml_dtypes.bfloat16


def bf(x):
    return np.asarray(x, np.float32).astype(BF16)


def f64(x):
    return np.asarray(x).astype(np.float64)


B, N, D, F, M1, M2 = 1, 128, 512, 512, 3, 5
EPS = 1e-12


def erf(z):
    a = np.clip(z, -6.0, 6.0)
    a2 = 2.0 * a * a
    term = a.copy()
    tot = a.copy()
    for k in range(1, 120):
        term = term * (a2 / (2 * k + 1))
        tot = tot + term
    return 2.0 / np.sqrt(np.pi) * np.exp(-a * a) * tot


def gelu(v):
    return 0.5 * v * (1.0 + erf(v / np.sqrt(2.0)))


def setup_inputs():
    s = mx_kscale(D)
    return {'x': bf(np.random.standard_normal((B, N, D, M1)) * s[:, None]),
            'w_in': bf(np.random.standard_normal((D, F)) / np.sqrt(D) / s[:, None]),
            'scale': bf(1.0 + 0.1 * np.random.standard_normal((1, 1, F))),
            'bias': bf(0.3 * np.random.standard_normal((1, 1, F))),
            'w_out': bf(np.random.standard_normal((F, D)) / np.sqrt(F))}


def reference(x, w_in, scale, bias, w_out):
    xq = mxq(f64(x), 2, 'e4m3')
    h = np.swapaxes(np.swapaxes(xq, -1, -2) @ mxq(f64(w_in), 0, 'e4m3'), -1, -2)
    norm = np.maximum(np.sqrt(np.sum(h * h, axis=-1, keepdims=True)), EPS)
    phase = h / norm
    gated = gelu(norm[..., 0] * f64(scale) + f64(bias))[..., None]
    g = gated * phase
    y = np.swapaxes(mxq(g, 2, 'e4m3'), -1, -2) @ mxq(f64(w_out), 0, 'e4m3')
    return np.swapaxes(y, -1, -2)

@@ -1,0 +1,188 @@
+from contextlib import ExitStack
+
+import concourse.mybir as mybir
+from concourse.masks import make_identity
+
+FP8X4 = mybir.dt.float8_e4m3fn_x4
+BF16 = mybir.dt.bfloat16
+F32 = mybir.dt.float32
+I32 = mybir.dt.int32
+U32 = mybir.dt.uint32
+U8 = mybir.dt.uint8
+ACT = mybir.ActivationFunctionType
+ALU = mybir.AluOpType
+
+P = 128
+PACK = 4
+CHANNELS = P * PACK
+COMPONENTS = 3
+EPS = 1e-12
+
+FLOPS = 2 * 2 * P * COMPONENTS * CHANNELS * CHANNELS
+
+
+def load_weight(nc, raw, w):
+    nc.sync.dma_start(out=raw, in_=w.rearrange("(t p) c -> p t c", p=P))
+
+
+def regroup_weight(nc, grouped, raw):
+    nc.vector.tensor_copy(
+        out=grouped.rearrange("p (c i) t -> p c t i", i=4),
+        in_=raw.rearrange("p t (c i) -> p c t i", i=4),
+    )
+
+
+def quantise(nc, codes, scales, grouped):
+    nc.vector.quantize_mx(
+        out=codes.bitcast(FP8X4),
+        scales=scales,
+        in_=grouped.rearrange("p c t -> p (c t)"),
+    )
+
+
+def tile_feedforwardse3_pa_s_kernel(tc, x, w_in, scale, bias, w_out, out):
+    nc = tc.nc
+    with ExitStack() as stack:
+        sbuf = stack.enter_context(tc.tile_pool(name="sbuf", bufs=1))
+        psum = stack.enter_context(tc.psum_pool(name="psum", bufs=1))
+        stack.enter_context(tc.manual_schedule())
+
+        x_sb = sbuf.tile([P, CHANNELS, COMPONENTS], BF16)
+        nc.sync.dma_start(out=x_sb[:], in_=x.rearrange("b n d m -> (b n) d m"))
+
+        gain_rows = sbuf.tile([P, P], BF16)
+        nc.vector.memset(gain_rows[:].bitcast(I32), 0)
+        nc.scalar.dma_start(
+            out=gain_rows[0:PACK, :], in_=scale.rearrange("a b (t p) -> (a b t) p", p=P)
+        )
+        nc.scalar.dma_start(
+            out=gain_rows[PACK : 2 * PACK, :], in_=bias.rearrange("a b (t p) -> (a b t) p", p=P)
+        )
+
+        w_in_raw = sbuf.tile([P, PACK, CHANNELS], BF16)
+        load_weight(nc, w_in_raw[:], w_in)
+        w_out_raw = sbuf.tile([P, PACK, CHANNELS], BF16)
+        load_weight(nc, w_out_raw[:], w_out)
+
+        identity = sbuf.tile([P, P], BF16)
+        make_identity(nc, identity[:])
+
+        one = sbuf.tile([P, 1], F32)
+        nc.vector.memset(one[:], 1.0)
+        table_warm = sbuf.tile([P, 1], F32)
+        nc.scalar.activation(out=table_warm[:], in_=one[:], func=ACT.Abs_reciprocal_sqrt)
+
+        x_grouped = sbuf.tile([P, COMPONENTS, P, PACK], BF16, align_bytes=64)
+        for m in range(COMPONENTS):
+            xT = psum.tile([P, PACK, P], BF16, name="xT%d" % m, tag="bank%d" % m)
+            for t in range(PACK):
+                nc.tensor.transpose(xT[:, t, :], x_sb[:, t * P : (t + 1) * P, m], identity[:])
+            nc.scalar.copy(out=x_grouped[:, m, :, :], in_=xT[:].rearrange("p t n -> p n t"))
+
+        gain_T = psum.tile([P, P], BF16, tag="bank3")
+        nc.tensor.transpose(gain_T[:], gain_rows[:], identity[:])
+        gain = sbuf.tile([P, 2 * PACK], F32)
+        nc.scalar.copy(out=gain[:], in_=gain_T[:, 0 : 2 * PACK])
+
+        w_in_grouped = sbuf.tile([P, CHANNELS, PACK], BF16, align_bytes=64)
+        w_in_codes = sbuf.tile([P, CHANNELS], U32, align_bytes=64)
+        w_in_scales = sbuf.tile([P, CHANNELS], U8, align_bytes=64)
+        x_codes = sbuf.tile([P, COMPONENTS, P], U32, align_bytes=64)
+        x_scales = sbuf.tile([P, COMPONENTS, P], U8, align_bytes=64)
+        regroup_weight(nc, w_in_grouped[:], w_in_raw[:])
+        quantise(nc, x_codes[:, 0, :], x_scales[:, 0, :], x_grouped[:, 0, :, :])
+        quantise(nc, w_in_codes[:], w_in_scales[:], w_in_grouped[:])
+        quantise(nc, x_codes[:, 1, :], x_scales[:, 1, :], x_grouped[:, 1, :, :])
+        quantise(nc, x_codes[:, 2, :], x_scales[:, 2, :], x_grouped[:, 2, :, :])
+
+        h = []
+        squares = sbuf.tile([P, COMPONENTS, PACK, P], F32)
+        for m in range(COMPONENTS):
+            h.append(psum.tile([P, PACK, P], F32, name="h%d" % m))
+            for t in range(PACK):
+                f_cols = slice(t * P, (t + 1) * P)
+                nc.tensor.matmul_mx(
+                    out=h[m][:, t, :],
+                    lhsT=w_in_codes[:, f_cols].bitcast(FP8X4),
+                    lhsT_scale=w_in_scales[:, f_cols],
+                    rhs=x_codes[:, m, :].bitcast(FP8X4),
+                    rhs_scale=x_scales[:, m, :],
+                    start=True,
+                    stop=True,
+                )
+            nc.scalar.activation(out=squares[:, m, :, :], in_=h[m][:], func=ACT.Square)
+
+        w_out_grouped = sbuf.tile([P, CHANNELS, PACK], BF16, align_bytes=64)
+        w_out_codes = sbuf.tile([P, CHANNELS], U32, align_bytes=64)
+        w_out_scales = sbuf.tile([P, CHANNELS], U8, align_bytes=64)
+        regroup_weight(nc, w_out_grouped[:], w_out_raw[:])
+        quantise(nc, w_out_codes[:], w_out_scales[:], w_out_grouped[:])
+
+        sum_two = sbuf.tile([P, PACK, P], F32)
+        sum_squares = sbuf.tile([P, PACK, P], F32)
+        nc.vector.tensor_add(out=sum_two[:], in0=squares[:, 0, :, :], in1=squares[:, 1, :, :])
+        nc.vector.tensor_add(out=sum_squares[:], in0=sum_two[:], in1=squares[:, 2, :, :])
+        inv_sqrt = sbuf.tile([P, PACK, P], F32)
+        nc.scalar.activation(out=inv_sqrt[:], in_=sum_squares[:], func=ACT.Abs_reciprocal_sqrt)
+        inv_norm = sbuf.tile([P, PACK, P], F32)
+        nc.vector.tensor_scalar_min(out=inv_norm[:], in0=inv_sqrt[:], scalar1=1.0 / EPS)
+        norm = sbuf.tile([P, PACK, P], F32)
+        nc.vector.scalar_tensor_tensor(
+            out=norm[:],
+            in0=sum_squares[:],
+            scalar=EPS * EPS,
+            in1=inv_norm[:],
+            op0=ALU.max,
+            op1=ALU.mult,
+        )
+        gated = sbuf.tile([P, PACK, P], F32)
+        factor = sbuf.tile([P, PACK, P], F32)
+        for t in range(PACK):
+            nc.scalar.activation(
+                out=gated[:, t, :],
+                in_=norm[:, t, :],
+                func=ACT.Gelu,
+                scale=gain[:, t : t + 1],
+                bias=gain[:, PACK + t : PACK + t + 1],
+            )
+            nc.vector.tensor_mul(out=factor[:, t, :], in0=gated[:, t, :], in1=inv_norm[:, t, :])
+
+        g_grouped = sbuf.tile([P, COMPONENTS, P, PACK], BF16, align_bytes=64)
+        g_codes = sbuf.tile([P, COMPONENTS, P], U32, align_bytes=64)
+        g_scales = sbuf.tile([P, COMPONENTS, P], U8, align_bytes=64)
+        y = [
+            psum.tile([P, COMPONENTS, P], F32, name="y%d" % j, tag="bank%d" % j)
+            for j in range(PACK)
+        ]
+        for step in range(COMPONENTS + 1):
+            if step < COMPONENTS:
+                nc.vector.tensor_mul(
+                    out=g_grouped[:, step, :, :],
+                    in0=h[step][:].rearrange("p t n -> p n t"),
+                    in1=factor[:].rearrange("p t n -> p n t"),
+                )
+            if step >= 1:
+                m = step - 1
+                quantise(nc, g_codes[:, m, :], g_scales[:, m, :], g_grouped[:, m, :, :])
+                for j in range(PACK):
+                    d_cols = slice(j * P, (j + 1) * P)
+                    nc.tensor.matmul_mx(
+                        out=y[j][:, m, :],
+                        lhsT=g_codes[:, m, :].bitcast(FP8X4),
+                        lhsT_scale=g_scales[:, m, :],
+                        rhs=w_out_codes[:, d_cols].bitcast(FP8X4),
+                        rhs_scale=w_out_scales[:, d_cols],
+                        start=True,
+                        stop=True,
+                    )
+
+        out_sb = sbuf.tile([P, CHANNELS, COMPONENTS], F32)
+        out_rows = out.rearrange("b n d m -> (b n) d m")
+        for j in range(PACK):
+            d_cols = slice(j * P, (j + 1) * P)
+            interleaved = y[j][:].rearrange("p m c -> p c m")
+            if j % 2 == 0:
+                nc.scalar.copy(out=out_sb[:, d_cols, :], in_=interleaved)
+            else:
+                nc.vector.tensor_copy(out=out_sb[:, d_cols, :], in_=interleaved)
+            nc.sync.dma_start(out=out_rows[:, d_cols, :], in_=out_sb[:, d_cols, :])

@@ -16,13 +16,12 @@ P = 128
 PACK = 4
 CHANNELS = P * PACK
 COMPONENTS = 3
+HALVES = 2
+HALF_BLOCKS = PACK // HALVES
+HALF_CHANNELS = CHANNELS // HALVES
 EPS = 1e-12
 
 FLOPS = 2 * 2 * P * COMPONENTS * CHANNELS * CHANNELS
-
-
-def load_weight(nc, raw, w):
-    nc.sync.dma_start(out=raw, in_=w.rearrange("(t p) c -> p t c", p=P))
 
 
 def regroup_weight(nc, grouped, raw):
@@ -33,11 +32,7 @@ def regroup_weight(nc, grouped, raw):
 
 
 def quantise(nc, codes, scales, grouped):
-    nc.vector.quantize_mx(
-        out=codes.bitcast(FP8X4),
-        scales=scales,
-        in_=grouped.rearrange("p c t -> p (c t)"),
-    )
+    nc.vector.quantize_mx(out=codes.bitcast(FP8X4), scales=scales, in_=grouped)
 
 
 def tile_feedforwardse3_pa_s_kernel(tc, x, w_in, scale, bias, w_out, out):
@@ -60,10 +55,18 @@ def tile_feedforwardse3_pa_s_kernel(tc, x, w_in, scale, bias, w_out, out):
         )
 
         w_in_raw = sbuf.tile([P, PACK, CHANNELS], BF16)
-        load_weight(nc, w_in_raw[:], w_in)
+        for half in range(HALVES):
+            f_cols = slice(half * HALF_CHANNELS, (half + 1) * HALF_CHANNELS)
+            for u in range(2):
+                nc.sync.dma_start(
+                    out=w_in_raw[:, 2 * u : 2 * u + 2, f_cols],
+                    in_=w_in[2 * P * u : 2 * P * (u + 1), f_cols].rearrange("(p e) c -> p e c", e=2),
+                )
         w_out_raw = sbuf.tile([P, PACK, CHANNELS], BF16)
-        load_weight(nc, w_out_raw[:], w_out)
+        nc.sync.dma_start(out=w_out_raw[:], in_=w_out.rearrange("(t p) c -> p t c", p=P))
 
+        identity_words = sbuf.tile([P, P], F32)
+        make_identity(nc, identity_words[:])
         identity = sbuf.tile([P, P], BF16)
         make_identity(nc, identity[:])
 
@@ -72,12 +75,22 @@ def tile_feedforwardse3_pa_s_kernel(tc, x, w_in, scale, bias, w_out, out):
         table_warm = sbuf.tile([P, 1], F32)
         nc.scalar.activation(out=table_warm[:], in_=one[:], func=ACT.Abs_reciprocal_sqrt)
 
-        x_grouped = sbuf.tile([P, COMPONENTS, P, PACK], BF16, align_bytes=64)
+        x_planes = sbuf.tile([P, COMPONENTS, CHANNELS], BF16)
         for m in range(COMPONENTS):
-            xT = psum.tile([P, PACK, P], BF16, name="xT%d" % m, tag="bank%d" % m)
-            for t in range(PACK):
-                nc.tensor.transpose(xT[:, t, :], x_sb[:, t * P : (t + 1) * P, m], identity[:])
-            nc.scalar.copy(out=x_grouped[:, m, :, :], in_=xT[:].rearrange("p t n -> p n t"))
+            if m % 2 == 0:
+                nc.vector.tensor_copy(out=x_planes[:, m, :], in_=x_sb[:, :, m])
+            else:
+                nc.scalar.copy(out=x_planes[:, m, :], in_=x_sb[:, :, m])
+        x_grouped = sbuf.tile([P, COMPONENTS, P * PACK], BF16, align_bytes=64)
+        for m in range(COMPONENTS):
+            xT = psum.tile([P, 2, P], F32, name="xT%d" % m, tag="bank%d" % m)
+            x_words = x_planes[:, m, :].bitcast(F32)
+            for u in range(2):
+                nc.tensor.transpose(xT[:, u, :], x_words[:, u * P : (u + 1) * P], identity_words[:])
+            nc.scalar.copy(
+                out=x_grouped[:, m, :].bitcast(F32).rearrange("p (n u) -> p n u", u=2),
+                in_=xT[:].rearrange("p u n -> p n u"),
+            )
 
         gain_T = psum.tile([P, P], BF16, tag="bank3")
         nc.tensor.transpose(gain_T[:], gain_rows[:], identity[:])
@@ -89,52 +102,91 @@ def tile_feedforwardse3_pa_s_kernel(tc, x, w_in, scale, bias, w_out, out):
         w_in_scales = sbuf.tile([P, CHANNELS], U8, align_bytes=64)
         x_codes = sbuf.tile([P, COMPONENTS, P], U32, align_bytes=64)
         x_scales = sbuf.tile([P, COMPONENTS, P], U8, align_bytes=64)
-        regroup_weight(nc, w_in_grouped[:], w_in_raw[:])
-        quantise(nc, x_codes[:, 0, :], x_scales[:, 0, :], x_grouped[:, 0, :, :])
-        quantise(nc, w_in_codes[:], w_in_scales[:], w_in_grouped[:])
-        quantise(nc, x_codes[:, 1, :], x_scales[:, 1, :], x_grouped[:, 1, :, :])
-        quantise(nc, x_codes[:, 2, :], x_scales[:, 2, :], x_grouped[:, 2, :, :])
 
-        h = []
-        squares = sbuf.tile([P, COMPONENTS, PACK, P], F32)
-        for m in range(COMPONENTS):
-            h.append(psum.tile([P, PACK, P], F32, name="h%d" % m))
-            for t in range(PACK):
-                f_cols = slice(t * P, (t + 1) * P)
-                nc.tensor.matmul_mx(
-                    out=h[m][:, t, :],
-                    lhsT=w_in_codes[:, f_cols].bitcast(FP8X4),
-                    lhsT_scale=w_in_scales[:, f_cols],
-                    rhs=x_codes[:, m, :].bitcast(FP8X4),
-                    rhs_scale=x_scales[:, m, :],
-                    start=True,
-                    stop=True,
-                )
-            nc.scalar.activation(out=squares[:, m, :, :], in_=h[m][:], func=ACT.Square)
+        def quantise_x(m):
+            quantise(nc, x_codes[:, m, :], x_scales[:, m, :], x_grouped[:, m, :])
+
+        def quantise_w_in(half):
+            f_cols = slice(half * HALF_CHANNELS, (half + 1) * HALF_CHANNELS)
+            quantise(
+                nc,
+                w_in_codes[:, f_cols],
+                w_in_scales[:, f_cols],
+                w_in_grouped[:, f_cols, :].rearrange("p c t -> p (c t)"),
+            )
+
+        for half in range(HALVES):
+            f_cols = slice(half * HALF_CHANNELS, (half + 1) * HALF_CHANNELS)
+            regroup_weight(nc, w_in_grouped[:, f_cols, :], w_in_raw[:, :, f_cols])
+        quantise_x(0)
+        quantise_w_in(0)
+        quantise_x(1)
+        quantise_x(2)
+        quantise_w_in(1)
 
         w_out_grouped = sbuf.tile([P, CHANNELS, PACK], BF16, align_bytes=64)
         w_out_codes = sbuf.tile([P, CHANNELS], U32, align_bytes=64)
         w_out_scales = sbuf.tile([P, CHANNELS], U8, align_bytes=64)
-        regroup_weight(nc, w_out_grouped[:], w_out_raw[:])
-        quantise(nc, w_out_codes[:], w_out_scales[:], w_out_grouped[:])
 
+        def regroup_w_out(half):
+            d_cols = slice(half * HALF_CHANNELS, (half + 1) * HALF_CHANNELS)
+            regroup_weight(nc, w_out_grouped[:, d_cols, :], w_out_raw[:, :, d_cols])
+
+        regroup_w_out(0)
+
+        h = [psum.tile([P, PACK, P], F32, name="h%d" % m) for m in range(COMPONENTS)]
+        squares = sbuf.tile([P, COMPONENTS, PACK, P], F32)
         sum_two = sbuf.tile([P, PACK, P], F32)
         sum_squares = sbuf.tile([P, PACK, P], F32)
-        nc.vector.tensor_add(out=sum_two[:], in0=squares[:, 0, :, :], in1=squares[:, 1, :, :])
-        nc.vector.tensor_add(out=sum_squares[:], in0=sum_two[:], in1=squares[:, 2, :, :])
+        for half in range(HALVES):
+            blocks = slice(half * HALF_BLOCKS, (half + 1) * HALF_BLOCKS)
+            for m in range(COMPONENTS):
+                for t in range(half * HALF_BLOCKS, (half + 1) * HALF_BLOCKS):
+                    f_cols = slice(t * P, (t + 1) * P)
+                    nc.tensor.matmul_mx(
+                        out=h[m][:, t, :],
+                        lhsT=w_in_codes[:, f_cols].bitcast(FP8X4),
+                        lhsT_scale=w_in_scales[:, f_cols],
+                        rhs=x_codes[:, m, :].bitcast(FP8X4),
+                        rhs_scale=x_scales[:, m, :],
+                        start=True,
+                        stop=True,
+                    )
+                nc.scalar.activation(
+                    out=squares[:, m, blocks, :], in_=h[m][:, blocks, :], func=ACT.Square
+                )
+            nc.vector.tensor_add(
+                out=sum_two[:, blocks, :], in0=squares[:, 0, blocks, :], in1=squares[:, 1, blocks, :]
+            )
+            nc.vector.tensor_add(
+                out=sum_squares[:, blocks, :], in0=sum_two[:, blocks, :], in1=squares[:, 2, blocks, :]
+            )
+
         inv_sqrt = sbuf.tile([P, PACK, P], F32)
-        nc.scalar.activation(out=inv_sqrt[:], in_=sum_squares[:], func=ACT.Abs_reciprocal_sqrt)
         inv_norm = sbuf.tile([P, PACK, P], F32)
-        nc.vector.tensor_scalar_min(out=inv_norm[:], in0=inv_sqrt[:], scalar1=1.0 / EPS)
         norm = sbuf.tile([P, PACK, P], F32)
-        nc.vector.scalar_tensor_tensor(
-            out=norm[:],
-            in0=sum_squares[:],
-            scalar=EPS * EPS,
-            in1=inv_norm[:],
-            op0=ALU.max,
-            op1=ALU.mult,
-        )
+        for half in range(HALVES):
+            blocks = slice(half * HALF_BLOCKS, (half + 1) * HALF_BLOCKS)
+            nc.scalar.activation(
+                out=inv_sqrt[:, blocks, :],
+                in_=sum_squares[:, blocks, :],
+                func=ACT.Abs_reciprocal_sqrt,
+            )
+            nc.vector.tensor_scalar_min(
+                out=inv_norm[:, blocks, :], in0=inv_sqrt[:, blocks, :], scalar1=1.0 / EPS
+            )
+            nc.vector.scalar_tensor_tensor(
+                out=norm[:, blocks, :],
+                in0=sum_squares[:, blocks, :],
+                scalar=EPS * EPS,
+                in1=inv_norm[:, blocks, :],
+                op0=ALU.max,
+                op1=ALU.mult,
+            )
+
+        regroup_w_out(1)
+        quantise(nc, w_out_codes[:], w_out_scales[:], w_out_grouped[:].rearrange("p c t -> p (c t)"))
+
         gated = sbuf.tile([P, PACK, P], F32)
         factor = sbuf.tile([P, PACK, P], F32)
         for t in range(PACK):
@@ -163,7 +215,12 @@ def tile_feedforwardse3_pa_s_kernel(tc, x, w_in, scale, bias, w_out, out):
                 )
             if step >= 1:
                 m = step - 1
-                quantise(nc, g_codes[:, m, :], g_scales[:, m, :], g_grouped[:, m, :, :])
+                quantise(
+                    nc,
+                    g_codes[:, m, :],
+                    g_scales[:, m, :],
+                    g_grouped[:, m, :, :].rearrange("p n t -> p (n t)"),
+                )
                 for j in range(PACK):
                     d_cols = slice(j * P, (j + 1) * P)
                     nc.tensor.matmul_mx(

@@ -55,13 +55,10 @@ def tile_feedforwardse3_pa_s_kernel(tc, x, w_in, scale, bias, w_out, out):
         )
 
         w_in_raw = sbuf.tile([P, PACK, CHANNELS], BF16)
-        for half in range(HALVES):
-            f_cols = slice(half * HALF_CHANNELS, (half + 1) * HALF_CHANNELS)
-            for u in range(2):
-                nc.sync.dma_start(
-                    out=w_in_raw[:, 2 * u : 2 * u + 2, f_cols],
-                    in_=w_in[2 * P * u : 2 * P * (u + 1), f_cols].rearrange("(p e) c -> p e c", e=2),
-                )
+        nc.sync.dma_start(
+            out=w_in_raw[:].rearrange("p (u e) c -> p u (e c)", e=2),
+            in_=w_in.rearrange("(u p e) c -> p u (e c)", p=P, e=2),
+        )
         w_out_raw = sbuf.tile([P, PACK, CHANNELS], BF16)
         nc.sync.dma_start(out=w_out_raw[:], in_=w_out.rearrange("(t p) c -> p t c", p=P))
 

@@ -14,20 +14,26 @@ ALU = mybir.AluOpType
 
 P = 128
 PACK = 4
+PAIR = 2
 CHANNELS = P * PACK
 COMPONENTS = 3
 HALVES = 2
 HALF_BLOCKS = PACK // HALVES
 HALF_CHANNELS = CHANNELS // HALVES
+RUN = 4
 EPS = 1e-12
 
 FLOPS = 2 * 2 * P * COMPONENTS * CHANNELS * CHANNELS
 
 
+def span(i, width):
+    return slice(i * width, (i + 1) * width)
+
+
 def regroup_weight(nc, grouped, raw):
     nc.vector.tensor_copy(
-        out=grouped.rearrange("p (c i) t -> p c t i", i=4),
-        in_=raw.rearrange("p t (c i) -> p c t i", i=4),
+        out=grouped.rearrange("p (c i) t -> p c t i", i=RUN),
+        in_=raw.rearrange("p t (c i) -> p c t i", i=RUN),
     )
 
 
@@ -45,27 +51,32 @@ def tile_feedforwardse3_pa_s_kernel(tc, x, w_in, scale, bias, w_out, out):
         x_sb = sbuf.tile([P, CHANNELS, COMPONENTS], BF16)
         nc.sync.dma_start(out=x_sb[:], in_=x.rearrange("b n d m -> (b n) d m"))
 
-        gain_rows = sbuf.tile([P, P], BF16)
-        nc.vector.memset(gain_rows[:].bitcast(I32), 0)
+        scale_bias_rows = sbuf.tile([P, P], BF16)
+        nc.vector.memset(scale_bias_rows[:].bitcast(I32), 0)
         nc.scalar.dma_start(
-            out=gain_rows[0:PACK, :], in_=scale.rearrange("a b (t p) -> (a b t) p", p=P)
+            out=scale_bias_rows[0:PACK, :], in_=scale.rearrange("a b (t p) -> (a b t) p", p=P)
         )
         nc.scalar.dma_start(
-            out=gain_rows[PACK : 2 * PACK, :], in_=bias.rearrange("a b (t p) -> (a b t) p", p=P)
+            out=scale_bias_rows[PACK : 2 * PACK, :],
+            in_=bias.rearrange("a b (t p) -> (a b t) p", p=P),
         )
 
         w_in_raw = sbuf.tile([P, PACK, CHANNELS], BF16)
-        nc.sync.dma_start(
-            out=w_in_raw[:].rearrange("p (u e) c -> p u (e c)", e=2),
-            in_=w_in.rearrange("(u p e) c -> p u (e c)", p=P, e=2),
-        )
+        for half in range(HALVES):
+            for u in range(PACK // PAIR):
+                nc.sync.dma_start(
+                    out=w_in_raw[:, span(u, PAIR), span(half, HALF_CHANNELS)],
+                    in_=w_in[span(u, PAIR * P), span(half, HALF_CHANNELS)].rearrange(
+                        "(p e) c -> p e c", e=PAIR
+                    ),
+                )
         w_out_raw = sbuf.tile([P, PACK, CHANNELS], BF16)
         nc.sync.dma_start(out=w_out_raw[:], in_=w_out.rearrange("(t p) c -> p t c", p=P))
 
         identity_words = sbuf.tile([P, P], F32)
         make_identity(nc, identity_words[:])
-        identity = sbuf.tile([P, P], BF16)
-        make_identity(nc, identity[:])
+        identity_bf16 = sbuf.tile([P, P], BF16)
+        make_identity(nc, identity_bf16[:])
 
         one = sbuf.tile([P, 1], F32)
         nc.vector.memset(one[:], 1.0)
@@ -80,19 +91,19 @@ def tile_feedforwardse3_pa_s_kernel(tc, x, w_in, scale, bias, w_out, out):
                 nc.scalar.copy(out=x_planes[:, m, :], in_=x_sb[:, :, m])
         x_grouped = sbuf.tile([P, COMPONENTS, P * PACK], BF16, align_bytes=64)
         for m in range(COMPONENTS):
-            xT = psum.tile([P, 2, P], F32, name="xT%d" % m, tag="bank%d" % m)
+            xT = psum.tile([P, PACK // PAIR, P], F32, name="xT%d" % m, tag="bank%d" % m)
             x_words = x_planes[:, m, :].bitcast(F32)
-            for u in range(2):
-                nc.tensor.transpose(xT[:, u, :], x_words[:, u * P : (u + 1) * P], identity_words[:])
+            for u in range(PACK // PAIR):
+                nc.tensor.transpose(xT[:, u, :], x_words[:, span(u, P)], identity_words[:])
             nc.scalar.copy(
-                out=x_grouped[:, m, :].bitcast(F32).rearrange("p (n u) -> p n u", u=2),
+                out=x_grouped[:, m, :].bitcast(F32).rearrange("p (n u) -> p n u", u=PACK // PAIR),
                 in_=xT[:].rearrange("p u n -> p n u"),
             )
 
-        gain_T = psum.tile([P, P], BF16, tag="bank3")
-        nc.tensor.transpose(gain_T[:], gain_rows[:], identity[:])
-        gain = sbuf.tile([P, 2 * PACK], F32)
-        nc.scalar.copy(out=gain[:], in_=gain_T[:, 0 : 2 * PACK])
+        scale_bias_T = psum.tile([P, P], BF16, tag="bank3")
+        nc.tensor.transpose(scale_bias_T[:], scale_bias_rows[:], identity_bf16[:])
+        scale_bias = sbuf.tile([P, 2 * PACK], F32)
+        nc.scalar.copy(out=scale_bias[:], in_=scale_bias_T[:, 0 : 2 * PACK])
 
         w_in_grouped = sbuf.tile([P, CHANNELS, PACK], BF16, align_bytes=64)
         w_in_codes = sbuf.tile([P, CHANNELS], U32, align_bytes=64)
@@ -104,17 +115,17 @@ def tile_feedforwardse3_pa_s_kernel(tc, x, w_in, scale, bias, w_out, out):
             quantise(nc, x_codes[:, m, :], x_scales[:, m, :], x_grouped[:, m, :])
 
         def quantise_w_in(half):
-            f_cols = slice(half * HALF_CHANNELS, (half + 1) * HALF_CHANNELS)
+            half_cols = span(half, HALF_CHANNELS)
             quantise(
                 nc,
-                w_in_codes[:, f_cols],
-                w_in_scales[:, f_cols],
-                w_in_grouped[:, f_cols, :].rearrange("p c t -> p (c t)"),
+                w_in_codes[:, half_cols],
+                w_in_scales[:, half_cols],
+                w_in_grouped[:, half_cols, :].rearrange("p c t -> p (c t)"),
             )
 
         for half in range(HALVES):
-            f_cols = slice(half * HALF_CHANNELS, (half + 1) * HALF_CHANNELS)
-            regroup_weight(nc, w_in_grouped[:, f_cols, :], w_in_raw[:, :, f_cols])
+            half_cols = span(half, HALF_CHANNELS)
+            regroup_weight(nc, w_in_grouped[:, half_cols, :], w_in_raw[:, :, half_cols])
         quantise_x(0)
         quantise_w_in(0)
         quantise_x(1)
@@ -126,8 +137,8 @@ def tile_feedforwardse3_pa_s_kernel(tc, x, w_in, scale, bias, w_out, out):
         w_out_scales = sbuf.tile([P, CHANNELS], U8, align_bytes=64)
 
         def regroup_w_out(half):
-            d_cols = slice(half * HALF_CHANNELS, (half + 1) * HALF_CHANNELS)
-            regroup_weight(nc, w_out_grouped[:, d_cols, :], w_out_raw[:, :, d_cols])
+            half_cols = span(half, HALF_CHANNELS)
+            regroup_weight(nc, w_out_grouped[:, half_cols, :], w_out_raw[:, :, half_cols])
 
         regroup_w_out(0)
 
@@ -136,14 +147,13 @@ def tile_feedforwardse3_pa_s_kernel(tc, x, w_in, scale, bias, w_out, out):
         sum_two = sbuf.tile([P, PACK, P], F32)
         sum_squares = sbuf.tile([P, PACK, P], F32)
         for half in range(HALVES):
-            blocks = slice(half * HALF_BLOCKS, (half + 1) * HALF_BLOCKS)
+            blocks = span(half, HALF_BLOCKS)
             for m in range(COMPONENTS):
                 for t in range(half * HALF_BLOCKS, (half + 1) * HALF_BLOCKS):
-                    f_cols = slice(t * P, (t + 1) * P)
                     nc.tensor.matmul_mx(
                         out=h[m][:, t, :],
-                        lhsT=w_in_codes[:, f_cols].bitcast(FP8X4),
-                        lhsT_scale=w_in_scales[:, f_cols],
+                        lhsT=w_in_codes[:, span(t, P)].bitcast(FP8X4),
+                        lhsT_scale=w_in_scales[:, span(t, P)],
                         rhs=x_codes[:, m, :].bitcast(FP8X4),
                         rhs_scale=x_scales[:, m, :],
                         start=True,
@@ -163,7 +173,7 @@ def tile_feedforwardse3_pa_s_kernel(tc, x, w_in, scale, bias, w_out, out):
         inv_norm = sbuf.tile([P, PACK, P], F32)
         norm = sbuf.tile([P, PACK, P], F32)
         for half in range(HALVES):
-            blocks = slice(half * HALF_BLOCKS, (half + 1) * HALF_BLOCKS)
+            blocks = span(half, HALF_BLOCKS)
             nc.scalar.activation(
                 out=inv_sqrt[:, blocks, :],
                 in_=sum_squares[:, blocks, :],
@@ -191,8 +201,8 @@ def tile_feedforwardse3_pa_s_kernel(tc, x, w_in, scale, bias, w_out, out):
                 out=gated[:, t, :],
                 in_=norm[:, t, :],
                 func=ACT.Gelu,
-                scale=gain[:, t : t + 1],
-                bias=gain[:, PACK + t : PACK + t + 1],
+                scale=scale_bias[:, t : t + 1],
+                bias=scale_bias[:, PACK + t : PACK + t + 1],
             )
             nc.vector.tensor_mul(out=factor[:, t, :], in0=gated[:, t, :], in1=inv_norm[:, t, :])
 
@@ -219,13 +229,12 @@ def tile_feedforwardse3_pa_s_kernel(tc, x, w_in, scale, bias, w_out, out):
                     g_grouped[:, m, :, :].rearrange("p n t -> p (n t)"),
                 )
                 for j in range(PACK):
-                    d_cols = slice(j * P, (j + 1) * P)
                     nc.tensor.matmul_mx(
                         out=y[j][:, m, :],
                         lhsT=g_codes[:, m, :].bitcast(FP8X4),
                         lhsT_scale=g_scales[:, m, :],
-                        rhs=w_out_codes[:, d_cols].bitcast(FP8X4),
-                        rhs_scale=w_out_scales[:, d_cols],
+                        rhs=w_out_codes[:, span(j, P)].bitcast(FP8X4),
+                        rhs_scale=w_out_scales[:, span(j, P)],
                         start=True,
                         stop=True,
                     )
@@ -233,10 +242,9 @@ def tile_feedforwardse3_pa_s_kernel(tc, x, w_in, scale, bias, w_out, out):
         out_sb = sbuf.tile([P, CHANNELS, COMPONENTS], F32)
         out_rows = out.rearrange("b n d m -> (b n) d m")
         for j in range(PACK):
-            d_cols = slice(j * P, (j + 1) * P)
             interleaved = y[j][:].rearrange("p m c -> p c m")
             if j % 2 == 0:
-                nc.scalar.copy(out=out_sb[:, d_cols, :], in_=interleaved)
+                nc.scalar.copy(out=out_sb[:, span(j, P), :], in_=interleaved)
             else:
-                nc.vector.tensor_copy(out=out_sb[:, d_cols, :], in_=interleaved)
-            nc.sync.dma_start(out=out_rows[:, d_cols, :], in_=out_sb[:, d_cols, :])
+                nc.vector.tensor_copy(out=out_sb[:, span(j, P), :], in_=interleaved)
+            nc.sync.dma_start(out=out_rows[:, span(j, P), :], in_=out_sb[:, span(j, P), :])

@@ -14,7 +14,6 @@ ALU = mybir.AluOpType
 
 P = 128
 PACK = 4
-PAIR = 2
 CHANNELS = P * PACK
 COMPONENTS = 3
 HALVES = 2
@@ -22,6 +21,7 @@ HALF_BLOCKS = PACK // HALVES
 HALF_CHANNELS = CHANNELS // HALVES
 RUN = 4
 EPS = 1e-12
+TINY = 1e-37
 
 FLOPS = 2 * 2 * P * COMPONENTS * CHANNELS * CHANNELS
 
@@ -63,18 +63,13 @@ def tile_feedforwardse3_pa_s_kernel(tc, x, w_in, scale, bias, w_out, out):
 
         w_in_raw = sbuf.tile([P, PACK, CHANNELS], BF16)
         for half in range(HALVES):
-            for u in range(PACK // PAIR):
-                nc.sync.dma_start(
-                    out=w_in_raw[:, span(u, PAIR), span(half, HALF_CHANNELS)],
-                    in_=w_in[span(u, PAIR * P), span(half, HALF_CHANNELS)].rearrange(
-                        "(p e) c -> p e c", e=PAIR
-                    ),
-                )
+            nc.sync.dma_start(
+                out=w_in_raw[:, :, span(half, HALF_CHANNELS)],
+                in_=w_in[:, span(half, HALF_CHANNELS)].rearrange("(p t) c -> p t c", t=PACK),
+            )
         w_out_raw = sbuf.tile([P, PACK, CHANNELS], BF16)
         nc.sync.dma_start(out=w_out_raw[:], in_=w_out.rearrange("(t p) c -> p t c", p=P))
 
-        identity_words = sbuf.tile([P, P], F32)
-        make_identity(nc, identity_words[:])
         identity_bf16 = sbuf.tile([P, P], BF16)
         make_identity(nc, identity_bf16[:])
 
@@ -83,27 +78,13 @@ def tile_feedforwardse3_pa_s_kernel(tc, x, w_in, scale, bias, w_out, out):
         table_warm = sbuf.tile([P, 1], F32)
         nc.scalar.activation(out=table_warm[:], in_=one[:], func=ACT.Abs_reciprocal_sqrt)
 
-        x_planes = sbuf.tile([P, COMPONENTS, CHANNELS], BF16)
+        x_grouped = sbuf.tile([P, COMPONENTS, P, PACK], BF16, align_bytes=64)
+        x_by_word = x_sb[:].rearrange("n (p t) m -> n t m p", t=PACK)
         for m in range(COMPONENTS):
-            if m % 2 == 0:
-                nc.vector.tensor_copy(out=x_planes[:, m, :], in_=x_sb[:, :, m])
-            else:
-                nc.scalar.copy(out=x_planes[:, m, :], in_=x_sb[:, :, m])
-        x_grouped = sbuf.tile([P, COMPONENTS, P * PACK], BF16, align_bytes=64)
-        for m in range(COMPONENTS):
-            xT = psum.tile([P, PACK // PAIR, P], F32, name="xT%d" % m, tag="bank%d" % m)
-            x_words = x_planes[:, m, :].bitcast(F32)
-            for u in range(PACK // PAIR):
-                nc.tensor.transpose(xT[:, u, :], x_words[:, span(u, P)], identity_words[:])
-            nc.scalar.copy(
-                out=x_grouped[:, m, :].bitcast(F32).rearrange("p (n u) -> p n u", u=PACK // PAIR),
-                in_=xT[:].rearrange("p u n -> p n u"),
-            )
-
-        scale_bias_T = psum.tile([P, P], BF16, tag="bank3")
-        nc.tensor.transpose(scale_bias_T[:], scale_bias_rows[:], identity_bf16[:])
-        scale_bias = sbuf.tile([P, 2 * PACK], F32)
-        nc.scalar.copy(out=scale_bias[:], in_=scale_bias_T[:, 0 : 2 * PACK])
+            xT = psum.tile([P, PACK, P], BF16, name="xT%d" % m, tag="bank%d" % (5 + m))
+            for t in range(PACK):
+                nc.tensor.transpose(xT[:, t, :], x_by_word[:, t, m, :], identity_bf16[:])
+            nc.scalar.copy(out=x_grouped[:, m, :, :], in_=xT[:].rearrange("p t n -> p n t"))
 
         w_in_grouped = sbuf.tile([P, CHANNELS, PACK], BF16, align_bytes=64)
         w_in_codes = sbuf.tile([P, CHANNELS], U32, align_bytes=64)
@@ -112,7 +93,12 @@ def tile_feedforwardse3_pa_s_kernel(tc, x, w_in, scale, bias, w_out, out):
         x_scales = sbuf.tile([P, COMPONENTS, P], U8, align_bytes=64)
 
         def quantise_x(m):
-            quantise(nc, x_codes[:, m, :], x_scales[:, m, :], x_grouped[:, m, :])
+            quantise(
+                nc,
+                x_codes[:, m, :],
+                x_scales[:, m, :],
+                x_grouped[:, m, :, :].rearrange("p n t -> p (n t)"),
+            )
 
         def quantise_w_in(half):
             half_cols = span(half, HALF_CHANNELS)
@@ -123,121 +109,200 @@ def tile_feedforwardse3_pa_s_kernel(tc, x, w_in, scale, bias, w_out, out):
                 w_in_grouped[:, half_cols, :].rearrange("p c t -> p (c t)"),
             )
 
-        for half in range(HALVES):
-            half_cols = span(half, HALF_CHANNELS)
-            regroup_weight(nc, w_in_grouped[:, half_cols, :], w_in_raw[:, :, half_cols])
-        quantise_x(0)
-        quantise_w_in(0)
-        quantise_x(1)
-        quantise_x(2)
-        quantise_w_in(1)
+        def regroup_w_in(cols):
+            regroup_weight(nc, w_in_grouped[:, cols, :], w_in_raw[:, :, cols])
 
         w_out_grouped = sbuf.tile([P, CHANNELS, PACK], BF16, align_bytes=64)
         w_out_codes = sbuf.tile([P, CHANNELS], U32, align_bytes=64)
         w_out_scales = sbuf.tile([P, CHANNELS], U8, align_bytes=64)
 
-        def regroup_w_out(half):
+        def regroup_w_out(cols):
+            regroup_weight(nc, w_out_grouped[:, cols, :], w_out_raw[:, :, cols])
+
+        def quantise_w_out(half):
             half_cols = span(half, HALF_CHANNELS)
-            regroup_weight(nc, w_out_grouped[:, half_cols, :], w_out_raw[:, :, half_cols])
+            quantise(
+                nc,
+                w_out_codes[:, half_cols],
+                w_out_scales[:, half_cols],
+                w_out_grouped[:, half_cols, :].rearrange("p c t -> p (c t)"),
+            )
 
-        regroup_w_out(0)
+        regroup_w_in(span(0, HALF_CHANNELS))
+        regroup_w_in(span(2, P))
+        quantise_w_in(0)
+        quantise_x(0)
+        regroup_w_in(span(3, P))
+        quantise_x(1)
+        quantise_w_in(1)
+        quantise_x(2)
+        regroup_w_out(span(0, HALF_CHANNELS))
 
-        h = [psum.tile([P, PACK, P], F32, name="h%d" % m) for m in range(COMPONENTS)]
+        h = [
+            [
+                psum.tile(
+                    [P, HALF_BLOCKS, P], F32, name="h%d%d" % (m, half), tag="bank%d" % (HALVES * m + half)
+                )
+                for half in range(HALVES)
+            ]
+            for m in range(COMPONENTS)
+        ]
         squares = sbuf.tile([P, COMPONENTS, PACK, P], F32)
         sum_two = sbuf.tile([P, PACK, P], F32)
         sum_squares = sbuf.tile([P, PACK, P], F32)
-        for half in range(HALVES):
-            blocks = span(half, HALF_BLOCKS)
-            for m in range(COMPONENTS):
-                for t in range(half * HALF_BLOCKS, (half + 1) * HALF_BLOCKS):
-                    nc.tensor.matmul_mx(
-                        out=h[m][:, t, :],
-                        lhsT=w_in_codes[:, span(t, P)].bitcast(FP8X4),
-                        lhsT_scale=w_in_scales[:, span(t, P)],
-                        rhs=x_codes[:, m, :].bitcast(FP8X4),
-                        rhs_scale=x_scales[:, m, :],
-                        start=True,
-                        stop=True,
-                    )
-                nc.scalar.activation(
-                    out=squares[:, m, blocks, :], in_=h[m][:, blocks, :], func=ACT.Square
-                )
+        inv_sqrt = sbuf.tile([P, PACK, P], F32)
+        norm = sbuf.tile([P, PACK, P], F32)
+
+        def first_matmul(m, t):
+            nc.tensor.matmul_mx(
+                out=h[m][t // HALF_BLOCKS][:, t % HALF_BLOCKS, :],
+                lhsT=w_in_codes[:, span(t, P)].bitcast(FP8X4),
+                lhsT_scale=w_in_scales[:, span(t, P)],
+                rhs=x_codes[:, m, :].bitcast(FP8X4),
+                rhs_scale=x_scales[:, m, :],
+                start=True,
+                stop=True,
+            )
+
+        def square(m, blocks):
+            half = blocks.start // HALF_BLOCKS
+            in_bank = slice(blocks.start - half * HALF_BLOCKS, blocks.stop - half * HALF_BLOCKS)
+            nc.scalar.activation(
+                out=squares[:, m, blocks, :], in_=h[m][half][:, in_bank, :], func=ACT.Square
+            )
+
+        def add_first_two(blocks):
             nc.vector.tensor_add(
                 out=sum_two[:, blocks, :], in0=squares[:, 0, blocks, :], in1=squares[:, 1, blocks, :]
             )
-            nc.vector.tensor_add(
-                out=sum_squares[:, blocks, :], in0=sum_two[:, blocks, :], in1=squares[:, 2, blocks, :]
+
+        def add_third(blocks):
+            nc.vector.scalar_tensor_tensor(
+                out=sum_squares[:, blocks, :],
+                in0=squares[:, 2, blocks, :],
+                scalar=TINY,
+                in1=sum_two[:, blocks, :],
+                op0=ALU.max,
+                op1=ALU.add,
             )
 
-        inv_sqrt = sbuf.tile([P, PACK, P], F32)
-        inv_norm = sbuf.tile([P, PACK, P], F32)
-        norm = sbuf.tile([P, PACK, P], F32)
-        for half in range(HALVES):
-            blocks = span(half, HALF_BLOCKS)
+        def inverse_root(blocks):
             nc.scalar.activation(
                 out=inv_sqrt[:, blocks, :],
                 in_=sum_squares[:, blocks, :],
                 func=ACT.Abs_reciprocal_sqrt,
             )
-            nc.vector.tensor_scalar_min(
-                out=inv_norm[:, blocks, :], in0=inv_sqrt[:, blocks, :], scalar1=1.0 / EPS
-            )
-            nc.vector.scalar_tensor_tensor(
+
+        def take_norm(blocks):
+            nc.gpsimd.tensor_tensor(
                 out=norm[:, blocks, :],
-                in0=sum_squares[:, blocks, :],
-                scalar=EPS * EPS,
-                in1=inv_norm[:, blocks, :],
-                op0=ALU.max,
+                in0=inv_sqrt[:, blocks, :],
+                in1=sum_squares[:, blocks, :],
+                op=ALU.mult,
+            )
+
+        phase = sbuf.tile([P, COMPONENTS, PACK, P], F32)
+
+        def take_phase(m, half):
+            blocks = span(half, HALF_BLOCKS)
+            nc.vector.scalar_tensor_tensor(
+                out=phase[:, m, blocks, :],
+                in0=inv_sqrt[:, blocks, :],
+                scalar=1.0 / EPS,
+                in1=h[m][half][:],
+                op0=ALU.min,
                 op1=ALU.mult,
             )
 
-        regroup_w_out(1)
-        quantise(nc, w_out_codes[:], w_out_scales[:], w_out_grouped[:].rearrange("p c t -> p (c t)"))
+        halves = [span(half, HALF_BLOCKS) for half in range(HALVES)]
+        last_pieces = [halves[0], slice(2, 3), slice(3, 4)]
+        for blocks in halves:
+            for m in range(COMPONENTS - 1):
+                for t in range(blocks.start, blocks.stop):
+                    first_matmul(m, t)
+                square(m, blocks)
+            add_first_two(blocks)
+            if blocks is halves[0]:
+                regroup_w_out(span(2, P))
+        for half in range(HALVES):
+            for t in range(half * HALF_BLOCKS, (half + 1) * HALF_BLOCKS):
+                first_matmul(COMPONENTS - 1, t)
+        for blocks in last_pieces:
+            square(COMPONENTS - 1, blocks)
+            add_third(blocks)
+
+        scale_bias_T = psum.tile([P, P], BF16, tag="bank6")
+        nc.tensor.transpose(scale_bias_T[:], scale_bias_rows[:], identity_bf16[:])
+        scale_bias = sbuf.tile([P, 2 * PACK], F32)
+        nc.scalar.copy(out=scale_bias[:], in_=scale_bias_T[:, 0 : 2 * PACK])
+
+        for blocks in last_pieces:
+            inverse_root(blocks)
+        for blocks in halves:
+            take_norm(blocks)
+        regroup_w_out(span(3, P))
+        quantise_w_out(0)
+        for m in range(COMPONENTS):
+            for half in range(HALVES):
+                take_phase(m, half)
+        quantise_w_out(1)
 
         gated = sbuf.tile([P, PACK, P], F32)
-        factor = sbuf.tile([P, PACK, P], F32)
-        for t in range(PACK):
-            nc.scalar.activation(
-                out=gated[:, t, :],
-                in_=norm[:, t, :],
-                func=ACT.Gelu,
-                scale=scale_bias[:, t : t + 1],
-                bias=scale_bias[:, PACK + t : PACK + t + 1],
-            )
-            nc.vector.tensor_mul(out=factor[:, t, :], in0=gated[:, t, :], in1=inv_norm[:, t, :])
+        token_halves = [span(i, P // 2) for i in range(2)]
+        for tokens in token_halves:
+            for t in range(PACK):
+                nc.scalar.activation(
+                    out=gated[:, t, tokens],
+                    in_=norm[:, t, tokens],
+                    func=ACT.Gelu,
+                    scale=scale_bias[:, t : t + 1],
+                    bias=scale_bias[:, PACK + t : PACK + t + 1],
+                )
 
         g_grouped = sbuf.tile([P, COMPONENTS, P, PACK], BF16, align_bytes=64)
         g_codes = sbuf.tile([P, COMPONENTS, P], U32, align_bytes=64)
         g_scales = sbuf.tile([P, COMPONENTS, P], U8, align_bytes=64)
+        y_banks = [6, 7, 0, 1]
         y = [
-            psum.tile([P, COMPONENTS, P], F32, name="y%d" % j, tag="bank%d" % j)
+            psum.tile([P, COMPONENTS, P], F32, name="y%d" % j, tag="bank%d" % y_banks[j])
             for j in range(PACK)
         ]
-        for step in range(COMPONENTS + 1):
-            if step < COMPONENTS:
-                nc.vector.tensor_mul(
-                    out=g_grouped[:, step, :, :],
-                    in0=h[step][:].rearrange("p t n -> p n t"),
-                    in1=factor[:].rearrange("p t n -> p n t"),
+
+        def multiply(m, tokens):
+            nc.vector.tensor_mul(
+                out=g_grouped[:, m, tokens, :],
+                in0=phase[:, m, :, tokens].rearrange("p t n -> p n t"),
+                in1=gated[:, :, tokens].rearrange("p t n -> p n t"),
+            )
+
+        def second_matmul(m):
+            quantise(
+                nc,
+                g_codes[:, m, :],
+                g_scales[:, m, :],
+                g_grouped[:, m, :, :].rearrange("p n t -> p (n t)"),
+            )
+            for j in range(PACK):
+                nc.tensor.matmul_mx(
+                    out=y[j][:, m, :],
+                    lhsT=g_codes[:, m, :].bitcast(FP8X4),
+                    lhsT_scale=g_scales[:, m, :],
+                    rhs=w_out_codes[:, span(j, P)].bitcast(FP8X4),
+                    rhs_scale=w_out_scales[:, span(j, P)],
+                    start=True,
+                    stop=True,
                 )
-            if step >= 1:
-                m = step - 1
-                quantise(
-                    nc,
-                    g_codes[:, m, :],
-                    g_scales[:, m, :],
-                    g_grouped[:, m, :, :].rearrange("p n t -> p (n t)"),
-                )
-                for j in range(PACK):
-                    nc.tensor.matmul_mx(
-                        out=y[j][:, m, :],
-                        lhsT=g_codes[:, m, :].bitcast(FP8X4),
-                        lhsT_scale=g_scales[:, m, :],
-                        rhs=w_out_codes[:, span(j, P)].bitcast(FP8X4),
-                        rhs_scale=w_out_scales[:, span(j, P)],
-                        start=True,
-                        stop=True,
-                    )
+
+        first, second = token_halves
+        multiply(0, first)
+        multiply(1, first)
+        multiply(0, second)
+        multiply(1, second)
+        second_matmul(0)
+        multiply(2, first)
+        multiply(2, second)
+        second_matmul(1)
+        second_matmul(2)
 
         out_sb = sbuf.tile([P, CHANNELS, COMPONENTS], F32)
         out_rows = out.rearrange("b n d m -> (b n) d m")

@@ -241,15 +241,15 @@ def tile_feedforwardse3_pa_s_kernel(tc, x, w_in, scale, bias, w_out, out):
         for blocks in halves:
             take_norm(blocks)
         regroup_w_out(span(3, P))
-        quantise_w_out(0)
-        for m in range(COMPONENTS):
-            for half in range(HALVES):
+        for half in range(HALVES):
+            for m in range(COMPONENTS):
                 take_phase(m, half)
+        quantise_w_out(0)
         quantise_w_out(1)
 
         gated = sbuf.tile([P, PACK, P], F32)
-        token_halves = [span(i, P // 2) for i in range(2)]
-        for tokens in token_halves:
+        column_halves = [span(i, P // 2) for i in range(2)]
+        for tokens in column_halves:
             for t in range(PACK):
                 nc.scalar.activation(
                     out=gated[:, t, tokens],
@@ -275,41 +275,51 @@ def tile_feedforwardse3_pa_s_kernel(tc, x, w_in, scale, bias, w_out, out):
                 in1=gated[:, :, tokens].rearrange("p t n -> p n t"),
             )
 
-        def second_matmul(m):
+        def quantise_g(m):
             quantise(
                 nc,
                 g_codes[:, m, :],
                 g_scales[:, m, :],
                 g_grouped[:, m, :, :].rearrange("p n t -> p (n t)"),
             )
-            for j in range(PACK):
-                nc.tensor.matmul_mx(
-                    out=y[j][:, m, :],
-                    lhsT=g_codes[:, m, :].bitcast(FP8X4),
-                    lhsT_scale=g_scales[:, m, :],
-                    rhs=w_out_codes[:, span(j, P)].bitcast(FP8X4),
-                    rhs_scale=w_out_scales[:, span(j, P)],
-                    start=True,
-                    stop=True,
-                )
 
-        first, second = token_halves
+        def second_matmul(m, j):
+            nc.tensor.matmul_mx(
+                out=y[j][:, m, :],
+                lhsT=g_codes[:, m, :].bitcast(FP8X4),
+                lhsT_scale=g_scales[:, m, :],
+                rhs=w_out_codes[:, span(j, P)].bitcast(FP8X4),
+                rhs_scale=w_out_scales[:, span(j, P)],
+                start=True,
+                stop=True,
+            )
+
+        first, second = column_halves
         multiply(0, first)
         multiply(1, first)
         multiply(0, second)
         multiply(1, second)
-        second_matmul(0)
+        quantise_g(0)
         multiply(2, first)
         multiply(2, second)
-        second_matmul(1)
-        second_matmul(2)
+        quantise_g(1)
+        quantise_g(2)
+
+        for j in range(PACK):
+            second_matmul(0, j)
+        for blocks in halves:
+            for m in range(1, COMPONENTS):
+                for j in range(blocks.start, blocks.stop):
+                    second_matmul(m, j)
 
         out_sb = sbuf.tile([P, CHANNELS, COMPONENTS], F32)
         out_rows = out.rearrange("b n d m -> (b n) d m")
         for j in range(PACK):
-            interleaved = y[j][:].rearrange("p m c -> p c m")
-            if j % 2 == 0:
-                nc.scalar.copy(out=out_sb[:, span(j, P), :], in_=interleaved)
-            else:
-                nc.vector.tensor_copy(out=out_sb[:, span(j, P), :], in_=interleaved)
-            nc.sync.dma_start(out=out_rows[:, span(j, P), :], in_=out_sb[:, span(j, P), :])
+            for piece in column_halves if j == 0 else [slice(0, P)]:
+                channels = slice(j * P + piece.start, j * P + piece.stop)
+                interleaved = y[j][:, :, piece].rearrange("p m c -> p c m")
+                if j % 2 == 0:
+                    nc.scalar.copy(out=out_sb[:, channels, :], in_=interleaved)
+                else:
+                    nc.vector.tensor_copy(out=out_sb[:, channels, :], in_=interleaved)
+                nc.sync.dma_start(out=out_rows[:, channels, :], in_=out_sb[:, channels, :])

@@ -49,7 +49,10 @@ def tile_feedforwardse3_pa_s_kernel(tc, x, w_in, scale, bias, w_out, out):
         stack.enter_context(tc.manual_schedule())
 
         x_sb = sbuf.tile([P, CHANNELS, COMPONENTS], BF16)
-        nc.sync.dma_start(out=x_sb[:], in_=x.rearrange("b n d m -> (b n) d m"))
+        x_rows = x.rearrange("b n d m -> (b n) d m")
+        for half in range(HALVES):
+            half_channels = span(half, HALF_CHANNELS)
+            nc.sync.dma_start(out=x_sb[:, half_channels, :], in_=x_rows[:, half_channels, :])
 
         scale_bias_rows = sbuf.tile([P, P], BF16)
         nc.vector.memset(scale_bias_rows[:].bitcast(I32), 0)
@@ -65,7 +68,7 @@ def tile_feedforwardse3_pa_s_kernel(tc, x, w_in, scale, bias, w_out, out):
         for half in range(HALVES):
             nc.sync.dma_start(
                 out=w_in_raw[:, :, span(half, HALF_CHANNELS)],
-                in_=w_in[:, span(half, HALF_CHANNELS)].rearrange("(p t) c -> p t c", t=PACK),
+                in_=w_in[:, span(half, HALF_CHANNELS)].rearrange("(t p) c -> p t c", t=PACK),
             )
         w_out_raw = sbuf.tile([P, PACK, CHANNELS], BF16)
         nc.sync.dma_start(out=w_out_raw[:], in_=w_out.rearrange("(t p) c -> p t c", p=P))
@@ -79,11 +82,10 @@ def tile_feedforwardse3_pa_s_kernel(tc, x, w_in, scale, bias, w_out, out):
         nc.scalar.activation(out=table_warm[:], in_=one[:], func=ACT.Abs_reciprocal_sqrt)
 
         x_grouped = sbuf.tile([P, COMPONENTS, P, PACK], BF16, align_bytes=64)
-        x_by_word = x_sb[:].rearrange("n (p t) m -> n t m p", t=PACK)
         for m in range(COMPONENTS):
             xT = psum.tile([P, PACK, P], BF16, name="xT%d" % m, tag="bank%d" % (5 + m))
             for t in range(PACK):
-                nc.tensor.transpose(xT[:, t, :], x_by_word[:, t, m, :], identity_bf16[:])
+                nc.tensor.transpose(xT[:, t, :], x_sb[:, span(t, P), m], identity_bf16[:])
             nc.scalar.copy(out=x_grouped[:, m, :, :], in_=xT[:].rearrange("p t n -> p n t"))
 
         w_in_grouped = sbuf.tile([P, CHANNELS, PACK], BF16, align_bytes=64)

@@ -272,9 +272,9 @@ def tile_feedforwardse3_pa_s_kernel(tc, x, w_in, scale, bias, w_out, out):
 
         def multiply(m, tokens):
             nc.vector.tensor_mul(
-                out=g_grouped[:, m, tokens, :],
-                in0=phase[:, m, :, tokens].rearrange("p t n -> p n t"),
-                in1=gated[:, :, tokens].rearrange("p t n -> p n t"),
+                out=g_grouped[:, m, tokens, :].rearrange("p (n i) t -> p n t i", i=RUN),
+                in0=phase[:, m, :, tokens].rearrange("p t (n i) -> p n t i", i=RUN),
+                in1=gated[:, :, tokens].rearrange("p t (n i) -> p n t i", i=RUN),
             )
 
         def quantise_g(m):

@@ -19,6 +19,8 @@ COMPONENTS = 3
 HALVES = 2
 HALF_BLOCKS = PACK // HALVES
 HALF_CHANNELS = CHANNELS // HALVES
+PAIR = 2
+WARM_PASSES = 10
 RUN = 4
 EPS = 1e-12
 TINY = 1e-37
@@ -120,15 +122,6 @@ def tile_feedforwardse3_pa_s_kernel(tc, x, w_in, scale, bias, w_out, out):
 
         def regroup_w_out(cols):
             regroup_weight(nc, w_out_grouped[:, cols, :], w_out_raw[:, :, cols])
-
-        def quantise_w_out(half):
-            half_cols = span(half, HALF_CHANNELS)
-            quantise(
-                nc,
-                w_out_codes[:, half_cols],
-                w_out_scales[:, half_cols],
-                w_out_grouped[:, half_cols, :].rearrange("p c t -> p (c t)"),
-            )
 
         regroup_w_in(span(0, HALF_CHANNELS))
         regroup_w_in(span(2, P))
@@ -246,8 +239,19 @@ def tile_feedforwardse3_pa_s_kernel(tc, x, w_in, scale, bias, w_out, out):
         for half in range(HALVES):
             for m in range(COMPONENTS):
                 take_phase(m, half)
-        quantise_w_out(0)
-        quantise_w_out(1)
+        quantise(nc, w_out_codes[:], w_out_scales[:], w_out_grouped[:].rearrange("p c t -> p (c t)"))
+
+        warm_bank = psum.tile([P, PAIR * P], F32, tag="bank0")
+        for i in range(WARM_PASSES):
+            nc.tensor.matmul_mx(
+                out=warm_bank[:],
+                lhsT=w_in_codes[:, span(0, P)].bitcast(FP8X4),
+                lhsT_scale=w_in_scales[:, span(0, P)],
+                rhs=x_codes[:, 0:PAIR, :].rearrange("p m n -> p (m n)").bitcast(FP8X4),
+                rhs_scale=x_scales[:, 0:PAIR, :].rearrange("p m n -> p (m n)"),
+                start=True,
+                stop=True,
+            )
 
         gated = sbuf.tile([P, PACK, P], F32)
         column_halves = [span(i, P // 2) for i in range(2)]
@@ -264,7 +268,7 @@ def tile_feedforwardse3_pa_s_kernel(tc, x, w_in, scale, bias, w_out, out):
         g_grouped = sbuf.tile([P, COMPONENTS, P, PACK], BF16, align_bytes=64)
         g_codes = sbuf.tile([P, COMPONENTS, P], U32, align_bytes=64)
         g_scales = sbuf.tile([P, COMPONENTS, P], U8, align_bytes=64)
-        y_banks = [6, 7, 0, 1]
+        y_banks = [6, 7, 2, 3]
         y = [
             psum.tile([P, COMPONENTS, P], F32, name="y%d" % j, tag="bank%d" % y_banks[j])
             for j in range(PACK)
@@ -296,14 +300,11 @@ def tile_feedforwardse3_pa_s_kernel(tc, x, w_in, scale, bias, w_out, out):
                 stop=True,
             )
 
-        first, second = column_halves
-        multiply(0, first)
-        multiply(1, first)
-        multiply(0, second)
-        multiply(1, second)
+        for tokens in column_halves:
+            multiply(0, tokens)
+        multiply(1, slice(0, P))
         quantise_g(0)
-        multiply(2, first)
-        multiply(2, second)
+        multiply(2, slice(0, P))
         quantise_g(1)
         quantise_g(2)
 

@@ -104,13 +104,12 @@ def tile_feedforwardse3_pa_s_kernel(tc, x, w_in, scale, bias, w_out, out):
                 x_grouped[:, m, :, :].rearrange("p n t -> p (n t)"),
             )
 
-        def quantise_w_in(half):
-            half_cols = span(half, HALF_CHANNELS)
+        def quantise_w_in(cols):
             quantise(
                 nc,
-                w_in_codes[:, half_cols],
-                w_in_scales[:, half_cols],
-                w_in_grouped[:, half_cols, :].rearrange("p c t -> p (c t)"),
+                w_in_codes[:, cols],
+                w_in_scales[:, cols],
+                w_in_grouped[:, cols, :].rearrange("p c t -> p (c t)"),
             )
 
         def regroup_w_in(cols):
@@ -125,13 +124,14 @@ def tile_feedforwardse3_pa_s_kernel(tc, x, w_in, scale, bias, w_out, out):
 
         regroup_w_in(span(0, HALF_CHANNELS))
         regroup_w_in(span(2, P))
-        quantise_w_in(0)
+        quantise_w_in(span(0, HALF_CHANNELS))
         quantise_x(0)
         regroup_w_in(span(3, P))
         quantise_x(1)
-        quantise_w_in(1)
+        quantise_w_in(span(2, P))
+        quantise_w_in(span(3, P))
         quantise_x(2)
-        regroup_w_out(span(0, HALF_CHANNELS))
+        regroup_w_out(slice(0, 3 * P))
 
         h = [
             [
@@ -188,8 +188,9 @@ def tile_feedforwardse3_pa_s_kernel(tc, x, w_in, scale, bias, w_out, out):
                 func=ACT.Abs_reciprocal_sqrt,
             )
 
-        def take_norm(blocks):
-            nc.gpsimd.tensor_tensor(
+        def take_norm(engine, half):
+            blocks = span(half, HALF_BLOCKS)
+            engine.tensor_tensor(
                 out=norm[:, blocks, :],
                 in0=inv_sqrt[:, blocks, :],
                 in1=sum_squares[:, blocks, :],
@@ -218,7 +219,7 @@ def tile_feedforwardse3_pa_s_kernel(tc, x, w_in, scale, bias, w_out, out):
                 square(m, blocks)
             add_first_two(blocks)
             if blocks is halves[0]:
-                regroup_w_out(span(2, P))
+                regroup_w_out(span(3, P))
         for half in range(HALVES):
             for t in range(half * HALF_BLOCKS, (half + 1) * HALF_BLOCKS):
                 first_matmul(COMPONENTS - 1, t)
@@ -233,13 +234,13 @@ def tile_feedforwardse3_pa_s_kernel(tc, x, w_in, scale, bias, w_out, out):
 
         for blocks in last_pieces:
             inverse_root(blocks)
-        for blocks in halves:
-            take_norm(blocks)
-        regroup_w_out(span(3, P))
-        for half in range(HALVES):
-            for m in range(COMPONENTS):
-                take_phase(m, half)
+        take_norm(nc.gpsimd, 0)
         quantise(nc, w_out_codes[:], w_out_scales[:], w_out_grouped[:].rearrange("p c t -> p (c t)"))
+        for m in range(COMPONENTS):
+            take_phase(m, 0)
+        take_norm(nc.vector, 1)
+        for m in range(COMPONENTS):
+            take_phase(m, 1)
 
         warm_bank = psum.tile([P, PAIR * P], F32, tag="bank0")
         for i in range(WARM_PASSES):
@@ -303,16 +304,13 @@ def tile_feedforwardse3_pa_s_kernel(tc, x, w_in, scale, bias, w_out, out):
         for tokens in column_halves:
             multiply(0, tokens)
         multiply(1, slice(0, P))
-        quantise_g(0)
         multiply(2, slice(0, P))
-        quantise_g(1)
-        quantise_g(2)
+        for m in range(COMPONENTS):
+            quantise_g(m)
 
-        for j in range(PACK):
-            second_matmul(0, j)
-        for blocks in halves:
-            for m in range(1, COMPONENTS):
-                for j in range(blocks.start, blocks.stop):
+        for pair in range(PACK // PAIR):
+            for m in range(COMPONENTS):
+                for j in range(pair * PAIR, (pair + 1) * PAIR):
                     second_matmul(m, j)
 
         out_sb = sbuf.tile([P, CHANNELS, COMPONENTS], F32)

@@ -315,12 +315,23 @@ def tile_feedforwardse3_pa_s_kernel(tc, x, w_in, scale, bias, w_out, out):
 
         out_sb = sbuf.tile([P, CHANNELS, COMPONENTS], F32)
         out_rows = out.rearrange("b n d m -> (b n) d m")
-        for j in range(PACK):
-            for piece in column_halves if j == 0 else [slice(0, P)]:
-                channels = slice(j * P + piece.start, j * P + piece.stop)
-                interleaved = y[j][:, :, piece].rearrange("p m c -> p c m")
-                if j % 2 == 0:
-                    nc.scalar.copy(out=out_sb[:, channels, :], in_=interleaved)
-                else:
-                    nc.vector.tensor_copy(out=out_sb[:, channels, :], in_=interleaved)
-                nc.sync.dma_start(out=out_rows[:, channels, :], in_=out_sb[:, channels, :])
+
+        def copy_out(copy, j, piece):
+            copy(
+                out=out_sb[:, j * P + piece.start : j * P + piece.stop, :],
+                in_=y[j][:, :, piece].rearrange("p m c -> p c m"),
+            )
+
+        def store(channels):
+            nc.sync.dma_start(out=out_rows[:, channels, :], in_=out_sb[:, channels, :])
+
+        first, second = column_halves
+        copy_out(nc.scalar.copy, 0, first)
+        store(first)
+        copy_out(nc.scalar.copy, 0, second)
+        store(second)
+        copy_out(nc.vector.tensor_copy, 1, slice(0, P))
+        store(span(1, P))
+        copy_out(nc.scalar.copy, 2, slice(0, P))
+        copy_out(nc.vector.tensor_copy, 3, slice(0, P))
+        store(slice(2 * P, 4 * P))

from contextlib import ExitStack

import concourse.mybir as mybir
from concourse.masks import make_identity

FP8X4 = mybir.dt.float8_e4m3fn_x4
BF16 = mybir.dt.bfloat16
F32 = mybir.dt.float32
I32 = mybir.dt.int32
U32 = mybir.dt.uint32
U8 = mybir.dt.uint8
ACT = mybir.ActivationFunctionType
ALU = mybir.AluOpType

P = 128
PACK = 4
CHANNELS = P * PACK
COMPONENTS = 3
HALVES = 2
HALF_BLOCKS = PACK // HALVES
HALF_CHANNELS = CHANNELS // HALVES
PAIR = 2
WARM_PASSES = 10
RUN = 4
EPS = 1e-12
TINY = 1e-37

FLOPS = 2 * 2 * P * COMPONENTS * CHANNELS * CHANNELS


def span(i, width):
    return slice(i * width, (i + 1) * width)


def regroup_weight(nc, grouped, raw):
    nc.vector.tensor_copy(
        out=grouped.rearrange("p (c i) t -> p c t i", i=RUN),
        in_=raw.rearrange("p t (c i) -> p c t i", i=RUN),
    )


def quantise(nc, codes, scales, grouped):
    nc.vector.quantize_mx(out=codes.bitcast(FP8X4), scales=scales, in_=grouped)


def tile_feedforwardse3_pa_s_kernel(tc, x, w_in, scale, bias, w_out, out):
    nc = tc.nc
    with ExitStack() as stack:
        sbuf = stack.enter_context(tc.tile_pool(name="sbuf", bufs=1))
        psum = stack.enter_context(tc.psum_pool(name="psum", bufs=1))
        stack.enter_context(tc.manual_schedule())

        x_sb = sbuf.tile([P, CHANNELS, COMPONENTS], BF16)
        x_rows = x.rearrange("b n d m -> (b n) d m")
        for half in range(HALVES):
            half_channels = span(half, HALF_CHANNELS)
            nc.sync.dma_start(out=x_sb[:, half_channels, :], in_=x_rows[:, half_channels, :])

        scale_bias_rows = sbuf.tile([P, P], BF16)
        nc.vector.memset(scale_bias_rows[:].bitcast(I32), 0)
        nc.scalar.dma_start(
            out=scale_bias_rows[0:PACK, :], in_=scale.rearrange("a b (t p) -> (a b t) p", p=P)
        )
        nc.scalar.dma_start(
            out=scale_bias_rows[PACK : 2 * PACK, :],
            in_=bias.rearrange("a b (t p) -> (a b t) p", p=P),
        )

        w_in_raw = sbuf.tile([P, PACK, CHANNELS], BF16)
        for half in range(HALVES):
            nc.sync.dma_start(
                out=w_in_raw[:, :, span(half, HALF_CHANNELS)],
                in_=w_in[:, span(half, HALF_CHANNELS)].rearrange("(t p) c -> p t c", t=PACK),
            )
        w_out_raw = sbuf.tile([P, PACK, CHANNELS], BF16)
        nc.sync.dma_start(out=w_out_raw[:], in_=w_out.rearrange("(t p) c -> p t c", p=P))

        identity_bf16 = sbuf.tile([P, P], BF16)
        make_identity(nc, identity_bf16[:])

        one = sbuf.tile([P, 1], F32)
        nc.vector.memset(one[:], 1.0)
        table_warm = sbuf.tile([P, 1], F32)
        nc.scalar.activation(out=table_warm[:], in_=one[:], func=ACT.Abs_reciprocal_sqrt)

        x_grouped = sbuf.tile([P, COMPONENTS, P, PACK], BF16, align_bytes=64)
        for m in range(COMPONENTS):
            xT = psum.tile([P, PACK, P], BF16, name="xT%d" % m, tag="bank%d" % (5 + m))
            for t in range(PACK):
                nc.tensor.transpose(xT[:, t, :], x_sb[:, span(t, P), m], identity_bf16[:])
            nc.scalar.copy(out=x_grouped[:, m, :, :], in_=xT[:].rearrange("p t n -> p n t"))

        w_in_grouped = sbuf.tile([P, CHANNELS, PACK], BF16, align_bytes=64)
        w_in_codes = sbuf.tile([P, CHANNELS], U32, align_bytes=64)
        w_in_scales = sbuf.tile([P, CHANNELS], U8, align_bytes=64)
        x_codes = sbuf.tile([P, COMPONENTS, P], U32, align_bytes=64)
        x_scales = sbuf.tile([P, COMPONENTS, P], U8, align_bytes=64)

        def quantise_x(m):
            quantise(
                nc,
                x_codes[:, m, :],
                x_scales[:, m, :],
                x_grouped[:, m, :, :].rearrange("p n t -> p (n t)"),
            )

        def quantise_w_in(cols):
            quantise(
                nc,
                w_in_codes[:, cols],
                w_in_scales[:, cols],
                w_in_grouped[:, cols, :].rearrange("p c t -> p (c t)"),
            )

        def regroup_w_in(cols):
            regroup_weight(nc, w_in_grouped[:, cols, :], w_in_raw[:, :, cols])

        w_out_grouped = sbuf.tile([P, CHANNELS, PACK], BF16, align_bytes=64)
        w_out_codes = sbuf.tile([P, CHANNELS], U32, align_bytes=64)
        w_out_scales = sbuf.tile([P, CHANNELS], U8, align_bytes=64)

        def regroup_w_out(cols):
            regroup_weight(nc, w_out_grouped[:, cols, :], w_out_raw[:, :, cols])

        regroup_w_in(span(0, HALF_CHANNELS))
        regroup_w_in(span(2, P))
        quantise_w_in(span(0, HALF_CHANNELS))
        quantise_x(0)
        regroup_w_in(span(3, P))
        quantise_x(1)
        quantise_w_in(span(2, P))
        quantise_w_in(span(3, P))
        quantise_x(2)
        regroup_w_out(slice(0, 3 * P))

        h = [
            [
                psum.tile(
                    [P, HALF_BLOCKS, P], F32, name="h%d%d" % (m, half), tag="bank%d" % (HALVES * m + half)
                )
                for half in range(HALVES)
            ]
            for m in range(COMPONENTS)
        ]
        squares = sbuf.tile([P, COMPONENTS, PACK, P], F32)
        sum_two = sbuf.tile([P, PACK, P], F32)
        sum_squares = sbuf.tile([P, PACK, P], F32)
        inv_sqrt = sbuf.tile([P, PACK, P], F32)
        norm = sbuf.tile([P, PACK, P], F32)

        def first_matmul(m, t):
            nc.tensor.matmul_mx(
                out=h[m][t // HALF_BLOCKS][:, t % HALF_BLOCKS, :],
                lhsT=w_in_codes[:, span(t, P)].bitcast(FP8X4),
                lhsT_scale=w_in_scales[:, span(t, P)],
                rhs=x_codes[:, m, :].bitcast(FP8X4),
                rhs_scale=x_scales[:, m, :],
                start=True,
                stop=True,
            )

        def square(m, blocks):
            half = blocks.start // HALF_BLOCKS
            in_bank = slice(blocks.start - half * HALF_BLOCKS, blocks.stop - half * HALF_BLOCKS)
            nc.scalar.activation(
                out=squares[:, m, blocks, :], in_=h[m][half][:, in_bank, :], func=ACT.Square
            )

        def add_first_two(blocks):
            nc.vector.tensor_add(
                out=sum_two[:, blocks, :], in0=squares[:, 0, blocks, :], in1=squares[:, 1, blocks, :]
            )

        def add_third(blocks):
            nc.vector.scalar_tensor_tensor(
                out=sum_squares[:, blocks, :],
                in0=squares[:, 2, blocks, :],
                scalar=TINY,
                in1=sum_two[:, blocks, :],
                op0=ALU.max,
                op1=ALU.add,
            )

        def inverse_root(blocks):
            nc.scalar.activation(
                out=inv_sqrt[:, blocks, :],
                in_=sum_squares[:, blocks, :],
                func=ACT.Abs_reciprocal_sqrt,
            )

        def take_norm(engine, half):
            blocks = span(half, HALF_BLOCKS)
            engine.tensor_tensor(
                out=norm[:, blocks, :],
                in0=inv_sqrt[:, blocks, :],
                in1=sum_squares[:, blocks, :],
                op=ALU.mult,
            )

        phase = sbuf.tile([P, COMPONENTS, PACK, P], F32)

        def take_phase(m, half):
            blocks = span(half, HALF_BLOCKS)
            nc.vector.scalar_tensor_tensor(
                out=phase[:, m, blocks, :],
                in0=inv_sqrt[:, blocks, :],
                scalar=1.0 / EPS,
                in1=h[m][half][:],
                op0=ALU.min,
                op1=ALU.mult,
            )

        halves = [span(half, HALF_BLOCKS) for half in range(HALVES)]
        last_pieces = [halves[0], slice(2, 3), slice(3, 4)]
        for blocks in halves:
            for m in range(COMPONENTS - 1):
                for t in range(blocks.start, blocks.stop):
                    first_matmul(m, t)
                square(m, blocks)
            add_first_two(blocks)
            if blocks is halves[0]:
                regroup_w_out(span(3, P))
        for half in range(HALVES):
            for t in range(half * HALF_BLOCKS, (half + 1) * HALF_BLOCKS):
                first_matmul(COMPONENTS - 1, t)
        for blocks in last_pieces:
            square(COMPONENTS - 1, blocks)
            add_third(blocks)

        scale_bias_T = psum.tile([P, P], BF16, tag="bank6")
        nc.tensor.transpose(scale_bias_T[:], scale_bias_rows[:], identity_bf16[:])
        scale_bias = sbuf.tile([P, 2 * PACK], F32)
        nc.scalar.copy(out=scale_bias[:], in_=scale_bias_T[:, 0 : 2 * PACK])

        for blocks in last_pieces:
            inverse_root(blocks)
        take_norm(nc.gpsimd, 0)
        quantise(nc, w_out_codes[:], w_out_scales[:], w_out_grouped[:].rearrange("p c t -> p (c t)"))
        for m in range(COMPONENTS):
            take_phase(m, 0)
        take_norm(nc.vector, 1)
        for m in range(COMPONENTS):
            take_phase(m, 1)

        warm_bank = psum.tile([P, PAIR * P], F32, tag="bank0")
        for i in range(WARM_PASSES):
            nc.tensor.matmul_mx(
                out=warm_bank[:],
                lhsT=w_in_codes[:, span(0, P)].bitcast(FP8X4),
                lhsT_scale=w_in_scales[:, span(0, P)],
                rhs=x_codes[:, 0:PAIR, :].rearrange("p m n -> p (m n)").bitcast(FP8X4),
                rhs_scale=x_scales[:, 0:PAIR, :].rearrange("p m n -> p (m n)"),
                start=True,
                stop=True,
            )

        gated = sbuf.tile([P, PACK, P], F32)
        column_halves = [span(i, P // 2) for i in range(2)]
        for tokens in column_halves:
            for t in range(PACK):
                nc.scalar.activation(
                    out=gated[:, t, tokens],
                    in_=norm[:, t, tokens],
                    func=ACT.Gelu,
                    scale=scale_bias[:, t : t + 1],
                    bias=scale_bias[:, PACK + t : PACK + t + 1],
                )

        g_grouped = sbuf.tile([P, COMPONENTS, P, PACK], BF16, align_bytes=64)
        g_codes = sbuf.tile([P, COMPONENTS, P], U32, align_bytes=64)
        g_scales = sbuf.tile([P, COMPONENTS, P], U8, align_bytes=64)
        y_banks = [6, 7, 2, 3]
        y = [
            psum.tile([P, COMPONENTS, P], F32, name="y%d" % j, tag="bank%d" % y_banks[j])
            for j in range(PACK)
        ]

        def multiply(m, tokens):
            nc.vector.tensor_mul(
                out=g_grouped[:, m, tokens, :].rearrange("p (n i) t -> p n t i", i=RUN),
                in0=phase[:, m, :, tokens].rearrange("p t (n i) -> p n t i", i=RUN),
                in1=gated[:, :, tokens].rearrange("p t (n i) -> p n t i", i=RUN),
            )

        def quantise_g(m):
            quantise(
                nc,
                g_codes[:, m, :],
                g_scales[:, m, :],
                g_grouped[:, m, :, :].rearrange("p n t -> p (n t)"),
            )

        def second_matmul(m, j):
            nc.tensor.matmul_mx(
                out=y[j][:, m, :],
                lhsT=g_codes[:, m, :].bitcast(FP8X4),
                lhsT_scale=g_scales[:, m, :],
                rhs=w_out_codes[:, span(j, P)].bitcast(FP8X4),
                rhs_scale=w_out_scales[:, span(j, P)],
                start=True,
                stop=True,
            )

        for tokens in column_halves:
            multiply(0, tokens)
        multiply(1, slice(0, P))
        multiply(2, slice(0, P))
        for m in range(COMPONENTS):
            quantise_g(m)

        for pair in range(PACK // PAIR):
            for m in range(COMPONENTS):
                for j in range(pair * PAIR, (pair + 1) * PAIR):
                    second_matmul(m, j)

        out_sb = sbuf.tile([P, CHANNELS, COMPONENTS], F32)
        out_rows = out.rearrange("b n d m -> (b n) d m")

        def copy_out(copy, j, piece):
            copy(
                out=out_sb[:, j * P + piece.start : j * P + piece.stop, :],
                in_=y[j][:, :, piece].rearrange("p m c -> p c m"),
            )

        def store(channels):
            nc.sync.dma_start(out=out_rows[:, channels, :], in_=out_sb[:, channels, :])

        first, second = column_halves
        copy_out(nc.scalar.copy, 0, first)
        store(first)
        copy_out(nc.scalar.copy, 0, second)
        store(second)
        copy_out(nc.vector.tensor_copy, 1, slice(0, P))
        store(span(1, P))
        copy_out(nc.scalar.copy, 2, slice(0, P))
        copy_out(nc.vector.tensor_copy, 3, slice(0, P))
        store(slice(2 * P, 4 * P))
